import numpy as np
import ml_dtypes


def mxq(x, axis, fmt="e4m3"):
    dtype, down = {"e4m3": (ml_dtypes.float8_e4m3fn, 7), "e5m2": (ml_dtypes.float8_e5m2, 14)}[fmt]
    v = np.moveaxis(np.asarray(x, np.float32).astype(ml_dtypes.bfloat16).astype(np.float64), axis, -1)
    blocks = v.reshape(v.shape[:-1] + (-1, 32))
    amax = np.abs(blocks).max(-1, keepdims=True)
    byte = np.maximum(np.where(amax > 0, np.frexp(amax)[1] - 1 + 127, 0) - down, 1)
    scale = np.exp2(byte - 127.0)
    codes = (blocks / scale).astype(np.float32).astype(dtype).astype(np.float64)
    return np.moveaxis((codes * scale).reshape(v.shape), -1, axis)


WIDE = False


def mx_kscale(k):
    if not WIDE:
        return np.ones(k)
    levels = np.array([20, -20, 10, -10, 0])
    a = np.random.permutation(np.resize(levels, k // 512 * 4)).reshape(k // 512, 4)
    idx = np.arange(k)
    return np.exp2(a[idx // 512, idx % 128 // 32])


BF16 = ml_dtypes.bfloat16


def bf(x):
    return np.asarray(x, np.float32).astype(BF16)


def f64(x):
    return np.asarray(x).astype(np.float64)


B, K, D, H1, H2, C = 128, 4, 2048, 1024, 512, 64
N = B * K


def pre_activation(nf1, nf2, w1_0, w2_0):
    agg = nf2.reshape(nf1.shape[0], -1, nf1.shape[1]).mean(axis=1)
    return nf1 @ w2_0 + agg @ w1_0


def setup_inputs():
    u = mx_kscale(H1)
    nf1 = bf(np.random.standard_normal((N, D)))
    nf2 = bf(np.random.standard_normal((N * K, D)))
    w1_0 = bf(np.random.standard_normal((D, H1)) / np.sqrt(D))
    w2_00 = bf(np.random.standard_normal((D, H1)) / np.sqrt(D))
    g = bf(np.random.standard_normal((N, H1)) * np.exp2(np.random.randint(-12, 1, (N, 1))) * 16.0 * u)
    z = pre_activation(f64(nf1), f64(nf2), f64(w1_0), f64(w2_00))
    return {"nf1": nf1, "nf2": nf2, "w1_0": w1_0, "w2_0": bf(f64(w2_00) / u[None, :]),
            "z": np.asarray(z, np.float32), "grad_out": g}


def reference(nf1, nf2, w1_0, w2_0, z, grad_out):
    dz = f64(grad_out) * (f64(z) > 0.0)
    return mxq(dz, 1, "e5m2") @ mxq(f64(w2_0), 1, "e4m3").T

@@ -1,0 +1,129 @@
+from contextlib import ExitStack
+
+import concourse.mybir as mybir
+from concourse.masks import make_identity
+
+F32 = mybir.dt.float32
+BF16 = mybir.dt.bfloat16
+U32 = mybir.dt.uint32
+U8 = mybir.dt.uint8
+E4M3X4 = mybir.dt.float8_e4m3fn_x4
+E5M2X4 = mybir.dt.float8_e5m2_x4
+ALU = mybir.AluOpType
+
+P = 128
+NODES, FEATURES, D = 512, 1024, 2048
+K_PASS = 512
+PASSES = FEATURES // K_PASS
+HALVES = 2
+NODE_TILES = NODES // P
+CHUNK = 512
+CHUNKS = D // CHUNK
+ROWS = CHUNK // P
+WORDS = FEATURES // 2
+
+FLOPS = 2 * NODES * D * FEATURES
+BYTES = D * FEATURES * 2 + NODES * FEATURES * (4 + 2) + NODES * D * 4
+
+
+def tile_graphsage_pa_v_kernel(tc, nf1, nf2, w1_0, w2_0, z, grad_out, out):
+    nc = tc.nc
+    with ExitStack() as ctx:
+        keep = ctx.enter_context(tc.tile_pool(name="keep", bufs=1))
+        turned = ctx.enter_context(tc.psum_pool(name="turned", bufs=4))
+        sums = ctx.enter_context(tc.psum_pool(name="sums", bufs=4))
+
+        identity = keep.tile([P, P], F32, name="identity")
+        make_identity(nc, identity[:])
+
+        z_raw, g_raw, w_raw = [], [], []
+        for i in range(NODE_TILES):
+            node_rows = slice(i * P, (i + 1) * P)
+            z_raw.append(keep.tile([P, FEATURES], F32, name="z_raw%d" % i))
+            nc.sync.dma_start(out=z_raw[i][:], in_=z[node_rows, :])
+            g_raw.append(keep.tile([P, FEATURES], BF16, name="g_raw%d" % i))
+            nc.sync.dma_start(out=g_raw[i][:], in_=grad_out[node_rows, :])
+            w_raw.append(keep.tile([P, ROWS * FEATURES], BF16, name="w_raw%d" % i))
+            nc.sync.dma_start(
+                out=w_raw[i][:],
+                in_=w2_0[i * CHUNK : (i + 1) * CHUNK, :].rearrange("(p t) k -> p (t k)", t=ROWS),
+            )
+
+        dz_codes = [keep.tile([P, PASSES, P], U32, name="dz_codes%d" % n, align_bytes=64) for n in range(NODE_TILES)]
+        dz_scales = [keep.tile([P, PASSES, P], U8, name="dz_scales%d" % n, align_bytes=64) for n in range(NODE_TILES)]
+        w_codes = [keep.tile([P, PASSES, CHUNK], U32, name="w_codes%d" % c, align_bytes=64) for c in range(CHUNKS)]
+        w_scales = [keep.tile([P, PASSES, CHUNK], U8, name="w_scales%d" % c, align_bytes=64) for c in range(CHUNKS)]
+
+        def prepare_nodes(n):
+            dz = keep.tile([P, FEATURES], BF16, name="dz%d" % n)
+            nc.vector.scalar_tensor_tensor(
+                out=dz[:], in0=z_raw[n][:], scalar=0.0, in1=g_raw[n][:], op0=ALU.is_gt, op1=ALU.mult
+            )
+            dz_words = dz[:].bitcast(F32)
+            bank = turned.tile([P, PASSES, HALVES, P], F32, name="bank", tag="bank")
+            for g in range(PASSES):
+                for u in range(HALVES):
+                    first = (g * HALVES + u) * P
+                    nc.tensor.transpose(bank[:, g, u, :], dz_words[:, first : first + P], identity[:])
+            grouped = keep.tile([P, PASSES * P * HALVES], F32, name="dz_grouped%d" % n, align_bytes=64)
+            nc.scalar.copy(
+                out=grouped[:].rearrange("p (g r u) -> p g r u", g=PASSES, u=HALVES),
+                in_=bank[:].rearrange("p g u r -> p g r u"),
+            )
+            nc.vector.quantize_mx(
+                out=dz_codes[n][:].rearrange("p g r -> p (g r)").bitcast(E5M2X4),
+                scales=dz_scales[n][:].rearrange("p g r -> p (g r)"),
+                in_=grouped[:].bitcast(BF16),
+            )
+
+        def prepare_weights(c):
+            w_words = w_raw[c][:].bitcast(F32)
+            for g in range(PASSES):
+                grouped = keep.tile([P, CHUNK * HALVES], F32, name="w_grouped%d_%d" % (c, g), align_bytes=64)
+                for pair in range(ROWS // 2):
+                    bank = turned.tile([P, 2, HALVES, P], F32, name="bank", tag="bank")
+                    for s in range(2):
+                        for u in range(HALVES):
+                            first = (pair * 2 + s) * WORDS + (g * HALVES + u) * P
+                            nc.tensor.transpose(bank[:, s, u, :], w_words[:, first : first + P], identity[:])
+                    span = slice(pair * 2 * P * HALVES, (pair + 1) * 2 * P * HALVES)
+                    copy = nc.vector.tensor_copy if (g == 0 and pair == 1) else nc.scalar.copy
+                    copy(
+                        out=grouped[:, span].rearrange("p (s r u) -> p s r u", s=2, u=HALVES),
+                        in_=bank[:].rearrange("p s u r -> p s r u"),
+                    )
+                nc.vector.quantize_mx(
+                    out=w_codes[c][:, g, :].bitcast(E4M3X4),
+                    scales=w_scales[c][:, g, :],
+                    in_=grouped[:].bitcast(BF16),
+                )
+
+        def multiply(pairs):
+            banks = [sums.tile([P, CHUNK], F32, name="acc", tag="acc") for pair in pairs]
+            for g in range(PASSES):
+                for acc, (n, c) in zip(banks, pairs):
+                    nc.tensor.matmul_mx(
+                        out=acc[:],
+                        lhsT=dz_codes[n][:, g, :].bitcast(E5M2X4),
+                        lhsT_scale=dz_scales[n][:, g, :],
+                        rhs=w_codes[c][:, g, :].bitcast(E4M3X4),
+                        rhs_scale=w_scales[c][:, g, :],
+                        start=(g == 0),
+                        stop=(g == PASSES - 1),
+                    )
+            for acc, (n, c) in zip(banks, pairs):
+                result = keep.tile([P, CHUNK], F32, name="result%d_%d" % (n, c))
+                copy = nc.vector.tensor_copy if (n + c) % 3 == 0 else nc.scalar.copy
+                copy(
+                    out=result[:].rearrange("p (r t) -> p r t", t=ROWS),
+                    in_=acc[:].rearrange("p (t r) -> p r t", t=ROWS),
+                )
+                nc.sync.dma_start(out=out[n * P : (n + 1) * P, c * CHUNK : (c + 1) * CHUNK], in_=result[:])
+
+        prepare_nodes(0)
+        for i in range(NODE_TILES):
+            prepare_weights(i)
+            multiply([(i, c) for c in range(i)])
+            if i + 1 < NODE_TILES:
+                prepare_nodes(i + 1)
+            multiply([(n, i) for n in range(i + 1)])

@@ -32,6 +32,7 @@ def tile_graphsage_pa_v_kernel(tc, nf1, nf2, w1_0, w2_0, z, grad_out, out):
         keep = ctx.enter_context(tc.tile_pool(name="keep", bufs=1))
         turned = ctx.enter_context(tc.psum_pool(name="turned", bufs=4))
         sums = ctx.enter_context(tc.psum_pool(name="sums", bufs=4))
+        ctx.enter_context(tc.manual_schedule())
 
         identity = keep.tile([P, P], F32, name="identity")
         make_identity(nc, identity[:])

@@ -39,28 +39,31 @@ def tile_graphsage_pa_v_kernel(tc, nf1, nf2, w1_0, w2_0, z, grad_out, out):
 
         z_raw, g_raw, w_raw = [], [], []
         for i in range(NODE_TILES):
-            node_rows = slice(i * P, (i + 1) * P)
-            z_raw.append(keep.tile([P, FEATURES], F32, name="z_raw%d" % i))
-            nc.sync.dma_start(out=z_raw[i][:], in_=z[node_rows, :])
-            g_raw.append(keep.tile([P, FEATURES], BF16, name="g_raw%d" % i))
-            nc.sync.dma_start(out=g_raw[i][:], in_=grad_out[node_rows, :])
             w_raw.append(keep.tile([P, ROWS * FEATURES], BF16, name="w_raw%d" % i))
             nc.sync.dma_start(
                 out=w_raw[i][:],
                 in_=w2_0[i * CHUNK : (i + 1) * CHUNK, :].rearrange("(p t) k -> p (t k)", t=ROWS),
             )
+            node_rows = slice(i * P, (i + 1) * P)
+            z_raw.append(keep.tile([P, FEATURES], F32, name="z_raw%d" % i))
+            nc.sync.dma_start(out=z_raw[i][:], in_=z[node_rows, :])
+            g_raw.append(keep.tile([P, FEATURES], BF16, name="g_raw%d" % i))
+            nc.sync.dma_start(out=g_raw[i][:], in_=grad_out[node_rows, :])
 
         dz_codes = [keep.tile([P, PASSES, P], U32, name="dz_codes%d" % n, align_bytes=64) for n in range(NODE_TILES)]
         dz_scales = [keep.tile([P, PASSES, P], U8, name="dz_scales%d" % n, align_bytes=64) for n in range(NODE_TILES)]
         w_codes = [keep.tile([P, PASSES, CHUNK], U32, name="w_codes%d" % c, align_bytes=64) for c in range(CHUNKS)]
         w_scales = [keep.tile([P, PASSES, CHUNK], U8, name="w_scales%d" % c, align_bytes=64) for c in range(CHUNKS)]
 
-        def prepare_nodes(n):
-            dz = keep.tile([P, FEATURES], BF16, name="dz%d" % n)
+        dz = [keep.tile([P, FEATURES], BF16, name="dz%d" % n) for n in range(NODE_TILES)]
+
+        def mask_nodes(n):
             nc.vector.scalar_tensor_tensor(
-                out=dz[:], in0=z_raw[n][:], scalar=0.0, in1=g_raw[n][:], op0=ALU.is_gt, op1=ALU.mult
+                out=dz[n][:], in0=z_raw[n][:], scalar=0.0, in1=g_raw[n][:], op0=ALU.is_gt, op1=ALU.mult
             )
-            dz_words = dz[:].bitcast(F32)
+
+        def prepare_nodes(n):
+            dz_words = dz[n][:].bitcast(F32)
             bank = turned.tile([P, PASSES, HALVES, P], F32, name="bank", tag="bank")
             for g in range(PASSES):
                 for u in range(HALVES):
@@ -88,8 +91,7 @@ def tile_graphsage_pa_v_kernel(tc, nf1, nf2, w1_0, w2_0, z, grad_out, out):
                             first = (pair * 2 + s) * WORDS + (g * HALVES + u) * P
                             nc.tensor.transpose(bank[:, s, u, :], w_words[:, first : first + P], identity[:])
                     span = slice(pair * 2 * P * HALVES, (pair + 1) * 2 * P * HALVES)
-                    copy = nc.vector.tensor_copy if (g == 0 and pair == 1) else nc.scalar.copy
-                    copy(
+                    nc.scalar.copy(
                         out=grouped[:, span].rearrange("p (s r u) -> p s r u", s=2, u=HALVES),
                         in_=bank[:].rearrange("p s u r -> p s r u"),
                     )
@@ -100,9 +102,9 @@ def tile_graphsage_pa_v_kernel(tc, nf1, nf2, w1_0, w2_0, z, grad_out, out):
                 )
 
         def multiply(pairs):
-            banks = [sums.tile([P, CHUNK], F32, name="acc", tag="acc") for pair in pairs]
-            for g in range(PASSES):
-                for acc, (n, c) in zip(banks, pairs):
+            for j, (n, c) in enumerate(pairs):
+                acc = sums.tile([P, CHUNK], F32, name="acc", tag="acc")
+                for g in range(PASSES):
                     nc.tensor.matmul_mx(
                         out=acc[:],
                         lhsT=dz_codes[n][:, g, :].bitcast(E5M2X4),
@@ -112,19 +114,19 @@ def tile_graphsage_pa_v_kernel(tc, nf1, nf2, w1_0, w2_0, z, grad_out, out):
                         start=(g == 0),
                         stop=(g == PASSES - 1),
                     )
-            for acc, (n, c) in zip(banks, pairs):
                 result = keep.tile([P, CHUNK], F32, name="result%d_%d" % (n, c))
-                copy = nc.vector.tensor_copy if (n + c) % 3 == 0 else nc.scalar.copy
+                copy = nc.vector.tensor_copy if j % 2 == 0 else nc.scalar.copy
                 copy(
                     out=result[:].rearrange("p (r t) -> p r t", t=ROWS),
                     in_=acc[:].rearrange("p (t r) -> p r t", t=ROWS),
                 )
                 nc.sync.dma_start(out=out[n * P : (n + 1) * P, c * CHUNK : (c + 1) * CHUNK], in_=result[:])
 
-        prepare_nodes(0)
+        mask_nodes(0)
+        prepare_weights(0)
         for i in range(NODE_TILES):
-            prepare_weights(i)
-            multiply([(i, c) for c in range(i)])
+            prepare_nodes(i)
             if i + 1 < NODE_TILES:
-                prepare_nodes(i + 1)
-            multiply([(n, i) for n in range(i + 1)])
+                mask_nodes(i + 1)
+                prepare_weights(i + 1)
+            multiply([(n, i) for n in range(i)] + [(i, c) for c in range(i + 1)])

@@ -115,7 +115,7 @@ def tile_graphsage_pa_v_kernel(tc, nf1, nf2, w1_0, w2_0, z, grad_out, out):
                         stop=(g == PASSES - 1),
                     )
                 result = keep.tile([P, CHUNK], F32, name="result%d_%d" % (n, c))
-                copy = nc.vector.tensor_copy if j % 2 == 0 else nc.scalar.copy
+                copy = nc.scalar.copy if 2 * j < len(pairs) else nc.vector.tensor_copy
                 copy(
                     out=result[:].rearrange("p (r t) -> p r t", t=ROWS),
                     in_=acc[:].rearrange("p (t r) -> p r t", t=ROWS),

@@ -37,13 +37,13 @@ def tile_graphsage_pa_v_kernel(tc, nf1, nf2, w1_0, w2_0, z, grad_out, out):
         identity = keep.tile([P, P], F32, name="identity")
         make_identity(nc, identity[:])
 
-        z_raw, g_raw, w_raw = [], [], []
+        z_raw, g_raw, w_raw = [], [], {}
         for i in range(NODE_TILES):
-            w_raw.append(keep.tile([P, ROWS * FEATURES], BF16, name="w_raw%d" % i))
-            nc.sync.dma_start(
-                out=w_raw[i][:],
-                in_=w2_0[i * CHUNK : (i + 1) * CHUNK, :].rearrange("(p t) k -> p (t k)", t=ROWS),
-            )
+            w_rows = w2_0[i * CHUNK : (i + 1) * CHUNK, :].rearrange("(p t) k -> p (t k)", t=ROWS)
+            for pair in range(ROWS // 2):
+                w_raw[i, pair] = keep.tile([P, 2 * FEATURES], BF16, name="w_raw%d_%d" % (i, pair))
+                span = slice(pair * 2 * FEATURES, (pair + 1) * 2 * FEATURES)
+                nc.sync.dma_start(out=w_raw[i, pair][:], in_=w_rows[:, span])
             node_rows = slice(i * P, (i + 1) * P)
             z_raw.append(keep.tile([P, FEATURES], F32, name="z_raw%d" % i))
             nc.sync.dma_start(out=z_raw[i][:], in_=z[node_rows, :])
@@ -55,12 +55,12 @@ def tile_graphsage_pa_v_kernel(tc, nf1, nf2, w1_0, w2_0, z, grad_out, out):
         w_codes = [keep.tile([P, PASSES, CHUNK], U32, name="w_codes%d" % c, align_bytes=64) for c in range(CHUNKS)]
         w_scales = [keep.tile([P, PASSES, CHUNK], U8, name="w_scales%d" % c, align_bytes=64) for c in range(CHUNKS)]
 
+        live = [keep.tile([P, FEATURES], BF16, name="live%d" % n) for n in range(NODE_TILES)]
         dz = [keep.tile([P, FEATURES], BF16, name="dz%d" % n) for n in range(NODE_TILES)]
 
         def mask_nodes(n):
-            nc.vector.scalar_tensor_tensor(
-                out=dz[n][:], in0=z_raw[n][:], scalar=0.0, in1=g_raw[n][:], op0=ALU.is_gt, op1=ALU.mult
-            )
+            nc.vector.tensor_scalar(out=live[n][:], in0=z_raw[n][:], scalar1=0.0, scalar2=None, op0=ALU.is_gt)
+            nc.vector.tensor_tensor(out=dz[n][:], in0=live[n][:], in1=g_raw[n][:], op=ALU.mult)
 
         def prepare_nodes(n):
             dz_words = dz[n][:].bitcast(F32)
@@ -81,24 +81,27 @@ def tile_graphsage_pa_v_kernel(tc, nf1, nf2, w1_0, w2_0, z, grad_out, out):
             )
 
         def prepare_weights(c):
-            w_words = w_raw[c][:].bitcast(F32)
-            for g in range(PASSES):
-                grouped = keep.tile([P, CHUNK * HALVES], F32, name="w_grouped%d_%d" % (c, g), align_bytes=64)
-                for pair in range(ROWS // 2):
+            grouped = [
+                keep.tile([P, CHUNK * HALVES], F32, name="w_grouped%d_%d" % (c, g), align_bytes=64) for g in range(PASSES)
+            ]
+            for pair in range(ROWS // 2):
+                w_words = w_raw[c, pair][:].bitcast(F32)
+                for g in range(PASSES):
                     bank = turned.tile([P, 2, HALVES, P], F32, name="bank", tag="bank")
                     for s in range(2):
                         for u in range(HALVES):
-                            first = (pair * 2 + s) * WORDS + (g * HALVES + u) * P
+                            first = s * WORDS + (g * HALVES + u) * P
                             nc.tensor.transpose(bank[:, s, u, :], w_words[:, first : first + P], identity[:])
                     span = slice(pair * 2 * P * HALVES, (pair + 1) * 2 * P * HALVES)
                     nc.scalar.copy(
-                        out=grouped[:, span].rearrange("p (s r u) -> p s r u", s=2, u=HALVES),
+                        out=grouped[g][:, span].rearrange("p (s r u) -> p s r u", s=2, u=HALVES),
                         in_=bank[:].rearrange("p s u r -> p s r u"),
                     )
+            for g in range(PASSES):
                 nc.vector.quantize_mx(
                     out=w_codes[c][:, g, :].bitcast(E4M3X4),
                     scales=w_scales[c][:, g, :],
-                    in_=grouped[:].bitcast(BF16),
+                    in_=grouped[g][:].bitcast(BF16),
                 )
 
         def multiply(pairs):

@@ -40,10 +40,13 @@ def tile_graphsage_pa_v_kernel(tc, nf1, nf2, w1_0, w2_0, z, grad_out, out):
         z_raw, g_raw, w_raw = [], [], {}
         for i in range(NODE_TILES):
             w_rows = w2_0[i * CHUNK : (i + 1) * CHUNK, :].rearrange("(p t) k -> p (t k)", t=ROWS)
-            for pair in range(ROWS // 2):
-                w_raw[i, pair] = keep.tile([P, 2 * FEATURES], BF16, name="w_raw%d_%d" % (i, pair))
-                span = slice(pair * 2 * FEATURES, (pair + 1) * 2 * FEATURES)
-                nc.sync.dma_start(out=w_raw[i, pair][:], in_=w_rows[:, span])
+            parts = 1 if i < 2 else 2
+            width = ROWS * FEATURES // parts
+            for part in range(parts):
+                w_part = keep.tile([P, width], BF16, name="w_raw%d_%d" % (i, part))
+                nc.sync.dma_start(out=w_part[:], in_=w_rows[:, part * width : (part + 1) * width])
+                for pair in range(2 // parts):
+                    w_raw[i, part + pair] = w_part[:, pair * 2 * FEATURES : (pair + 1) * 2 * FEATURES]
             node_rows = slice(i * P, (i + 1) * P)
             z_raw.append(keep.tile([P, FEATURES], F32, name="z_raw%d" % i))
             nc.sync.dma_start(out=z_raw[i][:], in_=z[node_rows, :])
@@ -85,7 +88,7 @@ def tile_graphsage_pa_v_kernel(tc, nf1, nf2, w1_0, w2_0, z, grad_out, out):
                 keep.tile([P, CHUNK * HALVES], F32, name="w_grouped%d_%d" % (c, g), align_bytes=64) for g in range(PASSES)
             ]
             for pair in range(ROWS // 2):
-                w_words = w_raw[c, pair][:].bitcast(F32)
+                w_words = w_raw[c, pair].bitcast(F32)
                 for g in range(PASSES):
                     bank = turned.tile([P, 2, HALVES, P], F32, name="bank", tag="bank")
                     for s in range(2):
@@ -118,7 +121,11 @@ def tile_graphsage_pa_v_kernel(tc, nf1, nf2, w1_0, w2_0, z, grad_out, out):
                         stop=(g == PASSES - 1),
                     )
                 result = keep.tile([P, CHUNK], F32, name="result%d_%d" % (n, c))
-                copy = nc.scalar.copy if 2 * j < len(pairs) else nc.vector.tensor_copy
+                if (NODE_TILES - 1, CHUNKS - 1) in pairs:
+                    on_vector = j == len(pairs) - 1
+                else:
+                    on_vector = 2 * j >= len(pairs)
+                copy = nc.vector.tensor_copy if on_vector else nc.scalar.copy
                 copy(
                     out=result[:].rearrange("p (r t) -> p r t", t=ROWS),
                     in_=acc[:].rearrange("p (t r) -> p r t", t=ROWS),

@@ -30,8 +30,7 @@ def tile_graphsage_pa_v_kernel(tc, nf1, nf2, w1_0, w2_0, z, grad_out, out):
     nc = tc.nc
     with ExitStack() as ctx:
         keep = ctx.enter_context(tc.tile_pool(name="keep", bufs=1))
-        turned = ctx.enter_context(tc.psum_pool(name="turned", bufs=4))
-        sums = ctx.enter_context(tc.psum_pool(name="sums", bufs=4))
+        banks = ctx.enter_context(tc.psum_pool(name="banks", bufs=8))
         ctx.enter_context(tc.manual_schedule())
 
         identity = keep.tile([P, P], F32, name="identity")
@@ -67,7 +66,7 @@ def tile_graphsage_pa_v_kernel(tc, nf1, nf2, w1_0, w2_0, z, grad_out, out):
 
         def prepare_nodes(n):
             dz_words = dz[n][:].bitcast(F32)
-            bank = turned.tile([P, PASSES, HALVES, P], F32, name="bank", tag="bank")
+            bank = banks.tile([P, PASSES, HALVES, P], F32, name="bank", tag="bank")
             for g in range(PASSES):
                 for u in range(HALVES):
                     first = (g * HALVES + u) * P
@@ -90,7 +89,7 @@ def tile_graphsage_pa_v_kernel(tc, nf1, nf2, w1_0, w2_0, z, grad_out, out):
             for pair in range(ROWS // 2):
                 w_words = w_raw[c, pair].bitcast(F32)
                 for g in range(PASSES):
-                    bank = turned.tile([P, 2, HALVES, P], F32, name="bank", tag="bank")
+                    bank = banks.tile([P, 2, HALVES, P], F32, name="bank", tag="bank")
                     for s in range(2):
                         for u in range(HALVES):
                             first = s * WORDS + (g * HALVES + u) * P
@@ -109,7 +108,7 @@ def tile_graphsage_pa_v_kernel(tc, nf1, nf2, w1_0, w2_0, z, grad_out, out):
 
         def multiply(pairs):
             for j, (n, c) in enumerate(pairs):
-                acc = sums.tile([P, CHUNK], F32, name="acc", tag="acc")
+                acc = banks.tile([P, CHUNK], F32, name="bank", tag="bank")
                 for g in range(PASSES):
                     nc.tensor.matmul_mx(
                         out=acc[:],

from contextlib import ExitStack

import concourse.mybir as mybir
from concourse.masks import make_identity

F32 = mybir.dt.float32
BF16 = mybir.dt.bfloat16
U32 = mybir.dt.uint32
U8 = mybir.dt.uint8
E4M3X4 = mybir.dt.float8_e4m3fn_x4
E5M2X4 = mybir.dt.float8_e5m2_x4
ALU = mybir.AluOpType

P = 128
NODES, FEATURES, D = 512, 1024, 2048
K_PASS = 512
PASSES = FEATURES // K_PASS
HALVES = 2
NODE_TILES = NODES // P
CHUNK = 512
CHUNKS = D // CHUNK
ROWS = CHUNK // P
WORDS = FEATURES // 2

FLOPS = 2 * NODES * D * FEATURES
BYTES = D * FEATURES * 2 + NODES * FEATURES * (4 + 2) + NODES * D * 4


def tile_graphsage_pa_v_kernel(tc, nf1, nf2, w1_0, w2_0, z, grad_out, out):
    nc = tc.nc
    with ExitStack() as ctx:
        keep = ctx.enter_context(tc.tile_pool(name="keep", bufs=1))
        banks = ctx.enter_context(tc.psum_pool(name="banks", bufs=8))
        ctx.enter_context(tc.manual_schedule())

        identity = keep.tile([P, P], F32, name="identity")
        make_identity(nc, identity[:])

        z_raw, g_raw, w_raw = [], [], {}
        for i in range(NODE_TILES):
            w_rows = w2_0[i * CHUNK : (i + 1) * CHUNK, :].rearrange("(p t) k -> p (t k)", t=ROWS)
            parts = 1 if i < 2 else 2
            width = ROWS * FEATURES // parts
            for part in range(parts):
                w_part = keep.tile([P, width], BF16, name="w_raw%d_%d" % (i, part))
                nc.sync.dma_start(out=w_part[:], in_=w_rows[:, part * width : (part + 1) * width])
                for pair in range(2 // parts):
                    w_raw[i, part + pair] = w_part[:, pair * 2 * FEATURES : (pair + 1) * 2 * FEATURES]
            node_rows = slice(i * P, (i + 1) * P)
            z_raw.append(keep.tile([P, FEATURES], F32, name="z_raw%d" % i))
            nc.sync.dma_start(out=z_raw[i][:], in_=z[node_rows, :])
            g_raw.append(keep.tile([P, FEATURES], BF16, name="g_raw%d" % i))
            nc.sync.dma_start(out=g_raw[i][:], in_=grad_out[node_rows, :])

        dz_codes = [keep.tile([P, PASSES, P], U32, name="dz_codes%d" % n, align_bytes=64) for n in range(NODE_TILES)]
        dz_scales = [keep.tile([P, PASSES, P], U8, name="dz_scales%d" % n, align_bytes=64) for n in range(NODE_TILES)]
        w_codes = [keep.tile([P, PASSES, CHUNK], U32, name="w_codes%d" % c, align_bytes=64) for c in range(CHUNKS)]
        w_scales = [keep.tile([P, PASSES, CHUNK], U8, name="w_scales%d" % c, align_bytes=64) for c in range(CHUNKS)]

        live = [keep.tile([P, FEATURES], BF16, name="live%d" % n) for n in range(NODE_TILES)]
        dz = [keep.tile([P, FEATURES], BF16, name="dz%d" % n) for n in range(NODE_TILES)]

        def mask_nodes(n):
            nc.vector.tensor_scalar(out=live[n][:], in0=z_raw[n][:], scalar1=0.0, scalar2=None, op0=ALU.is_gt)
            nc.vector.tensor_tensor(out=dz[n][:], in0=live[n][:], in1=g_raw[n][:], op=ALU.mult)

        def prepare_nodes(n):
            dz_words = dz[n][:].bitcast(F32)
            bank = banks.tile([P, PASSES, HALVES, P], F32, name="bank", tag="bank")
            for g in range(PASSES):
                for u in range(HALVES):
                    first = (g * HALVES + u) * P
                    nc.tensor.transpose(bank[:, g, u, :], dz_words[:, first : first + P], identity[:])
            grouped = keep.tile([P, PASSES * P * HALVES], F32, name="dz_grouped%d" % n, align_bytes=64)
            nc.scalar.copy(
                out=grouped[:].rearrange("p (g r u) -> p g r u", g=PASSES, u=HALVES),
                in_=bank[:].rearrange("p g u r -> p g r u"),
            )
            nc.vector.quantize_mx(
                out=dz_codes[n][:].rearrange("p g r -> p (g r)").bitcast(E5M2X4),
                scales=dz_scales[n][:].rearrange("p g r -> p (g r)"),
                in_=grouped[:].bitcast(BF16),
            )

        def prepare_weights(c):
            grouped = [
                keep.tile([P, CHUNK * HALVES], F32, name="w_grouped%d_%d" % (c, g), align_bytes=64) for g in range(PASSES)
            ]
            for pair in range(ROWS // 2):
                w_words = w_raw[c, pair].bitcast(F32)
                for g in range(PASSES):
                    bank = banks.tile([P, 2, HALVES, P], F32, name="bank", tag="bank")
                    for s in range(2):
                        for u in range(HALVES):
                            first = s * WORDS + (g * HALVES + u) * P
                            nc.tensor.transpose(bank[:, s, u, :], w_words[:, first : first + P], identity[:])
                    span = slice(pair * 2 * P * HALVES, (pair + 1) * 2 * P * HALVES)
                    nc.scalar.copy(
                        out=grouped[g][:, span].rearrange("p (s r u) -> p s r u", s=2, u=HALVES),
                        in_=bank[:].rearrange("p s u r -> p s r u"),
                    )
            for g in range(PASSES):
                nc.vector.quantize_mx(
                    out=w_codes[c][:, g, :].bitcast(E4M3X4),
                    scales=w_scales[c][:, g, :],
                    in_=grouped[g][:].bitcast(BF16),
                )

        def multiply(pairs):
            for j, (n, c) in enumerate(pairs):
                acc = banks.tile([P, CHUNK], F32, name="bank", tag="bank")
                for g in range(PASSES):
                    nc.tensor.matmul_mx(
                        out=acc[:],
                        lhsT=dz_codes[n][:, g, :].bitcast(E5M2X4),
                        lhsT_scale=dz_scales[n][:, g, :],
                        rhs=w_codes[c][:, g, :].bitcast(E4M3X4),
                        rhs_scale=w_scales[c][:, g, :],
                        start=(g == 0),
                        stop=(g == PASSES - 1),
                    )
                result = keep.tile([P, CHUNK], F32, name="result%d_%d" % (n, c))
                if (NODE_TILES - 1, CHUNKS - 1) in pairs:
                    on_vector = j == len(pairs) - 1
                else:
                    on_vector = 2 * j >= len(pairs)
                copy = nc.vector.tensor_copy if on_vector else nc.scalar.copy
                copy(
                    out=result[:].rearrange("p (r t) -> p r t", t=ROWS),
                    in_=acc[:].rearrange("p (t r) -> p r t", t=ROWS),
                )
                nc.sync.dma_start(out=out[n * P : (n + 1) * P, c * CHUNK : (c + 1) * CHUNK], in_=result[:])

        mask_nodes(0)
        prepare_weights(0)
        for i in range(NODE_TILES):
            prepare_nodes(i)
            if i + 1 < NODE_TILES:
                mask_nodes(i + 1)
                prepare_weights(i + 1)
            multiply([(n, i) for n in range(i)] + [(i, c) for c in range(i + 1)])
